import numpy as np
import ml_dtypes


def mxq(x, axis, fmt="e4m3"):
    dtype, down = {"e4m3": (ml_dtypes.float8_e4m3fn, 7), "e5m2": (ml_dtypes.float8_e5m2, 14)}[fmt]
    v = np.moveaxis(np.asarray(x, np.float32).astype(ml_dtypes.bfloat16).astype(np.float64), axis, -1)
    blocks = v.reshape(v.shape[:-1] + (-1, 32))
    amax = np.abs(blocks).max(-1, keepdims=True)
    byte = np.maximum(np.where(amax > 0, np.frexp(amax)[1] - 1 + 127, 0) - down, 1)
    scale = np.exp2(byte - 127.0)
    codes = (blocks / scale).astype(np.float32).astype(dtype).astype(np.float64)
    return np.moveaxis((codes * scale).reshape(v.shape), -1, axis)


WIDE = False


def mx_kscale(k):
    if not WIDE:
        return np.ones(k)
    levels = np.array([10, -10, 5, -5, 0])
    if k % 512:
        return np.exp2(np.random.permutation(np.resize(levels, k // 32))).repeat(32)
    a = np.empty((k // 512, 16))
    for p in range(k // 512):
        a[p, :8] = np.random.permutation(np.resize(levels, 8))
        for g in range(8):
            far = levels[np.abs(levels - a[p, g]) >= 10]
            a[p, g + 8] = far[np.random.randint(len(far))]
    return np.exp2(a.ravel()).repeat(32)


BF16 = ml_dtypes.bfloat16


def bf(x):
    return np.asarray(x, np.float32).astype(BF16)


def f64(x):
    return np.asarray(x).astype(np.float64)


B, HC, WC, C, F = 512, 2, 2, 512, 512


def preact(x_crop, W_r, W_i, b_r, b_i):
    sp = f64(x_crop)
    xr = sp[:, 0].transpose(1, 2, 0, 3)
    xi = sp[:, 1].transpose(1, 2, 0, 3)
    wr = f64(W_r)
    wi = f64(W_i)
    r = xr @ wr - xi @ wi + f64(b_r)
    i = xr @ wi + xi @ wr + f64(b_i)
    return np.stack([r.transpose(2, 0, 1, 3), i.transpose(2, 0, 1, 3)], axis=1)


def setup_inputs():
    s = mx_kscale(B)[:, None, None, None, None]
    u = mx_kscale(F)
    x0 = bf(np.stack([np.random.standard_normal((B, HC, WC, C)), np.random.standard_normal((B, HC, WC, C))], axis=1))
    W_r0 = bf(np.random.standard_normal((HC, WC, C, F)) * 0.5 / np.sqrt(C))
    W_i0 = bf(np.random.standard_normal((HC, WC, C, F)) * 0.5 / np.sqrt(C))
    b_r = bf(np.random.standard_normal(F) * 0.3)
    b_i = bf(np.random.standard_normal(F) * 0.3)
    g = bf(np.random.standard_normal((B, 2, HC, WC, F)) * np.exp2(np.random.randint(-6, 1, (B, 1, HC, WC, 1))) * 4.0 / s * u)
    z = preact(x0, W_r0, W_i0, b_r, b_i)
    return {"x_crop": bf(f64(x0) * s),
            "W_r": bf(f64(W_r0) / u),
            "W_i": bf(f64(W_i0) / u),
            "b_r": b_r,
            "b_i": b_i,
            "z": np.asarray(z, np.float32),
            "grad_out": g}


def reference(x_crop, W_r, W_i, b_r, b_i, z, grad_out):
    dz = f64(grad_out) * (f64(z) > 0.0)
    dzr = dz[:, 0].transpose(1, 2, 0, 3)
    dzi = dz[:, 1].transpose(1, 2, 0, 3)
    dr_f = mxq(dzr, 3, "e5m2")
    di_f = mxq(dzi, 3, "e5m2")
    wr = mxq(f64(W_r), 3, "e4m3").transpose(0, 1, 3, 2)
    wi = mxq(f64(W_i), 3, "e4m3").transpose(0, 1, 3, 2)
    rr = dr_f @ wr
    ii = di_f @ wi
    ri = dr_f @ wi
    ir = di_f @ wr
    gxr = rr + ii
    gxi = ir - ri
    dx = np.stack([gxr.transpose(2, 0, 1, 3), gxi.transpose(2, 0, 1, 3)], axis=1)
    dr_b = mxq(dzr, 2, "e5m2")
    di_b = mxq(dzi, 2, "e5m2")
    sp = f64(x_crop)
    xr = mxq(sp[:, 0].transpose(1, 2, 0, 3), 2, "e4m3").transpose(0, 1, 3, 2)
    xi = mxq(sp[:, 1].transpose(1, 2, 0, 3), 2, "e4m3").transpose(0, 1, 3, 2)
    dwr = (xr @ dr_b) + (xi @ di_b)
    return dx, dwr

@@ -1,0 +1,205 @@
+from contextlib import ExitStack
+
+import concourse.mybir as mybir
+from concourse.masks import make_identity
+
+F32 = mybir.dt.float32
+BF16 = mybir.dt.bfloat16
+U32 = mybir.dt.uint32
+U8 = mybir.dt.uint8
+E4 = mybir.dt.float8_e4m3fn_x4
+E5 = mybir.dt.float8_e5m2_x4
+ALU = mybir.AluOpType
+
+P = 128
+J = 4
+D = 512
+NPX = 4
+W4 = J * D
+
+FLOPS = 6 * NPX * 2 * D * D * D
+
+SCALAR_INTERLEAVES = (("x", 1),)
+
+
+def tile_dot_pa_v_kernel(tc, x_crop, W_r, W_i, b_r, b_i, z, grad_out, out_0, out_1):
+    nc = tc.nc
+    xv = x_crop.rearrange("(p j) r h w c -> p j r h w c", j=J)
+    gv = grad_out.rearrange("(p j) r h w f -> p j r h w f", j=J)
+    zv = z.rearrange("(p j) r h w f -> p j r h w f", j=J)
+    wv = (
+        W_r.rearrange("h w (p q) f -> p h w q f", q=J),
+        W_i.rearrange("h w (p q) f -> p h w q f", q=J),
+    )
+    o0v = out_0.rearrange("(p j) r h w c -> p j r h w c", j=J)
+    o1v = out_1.rearrange("h w (t m) f -> m h w t f", t=J)
+
+    with ExitStack() as ctx:
+        const = ctx.enter_context(tc.tile_pool(name="const", bufs=1))
+        zp = ctx.enter_context(tc.tile_pool(name="zp", bufs=4))
+        gp = ctx.enter_context(tc.tile_pool(name="gp", bufs=2))
+        xp = ctx.enter_context(tc.tile_pool(name="xp", bufs=2))
+        wp = ctx.enter_context(tc.tile_pool(name="wp", bufs=4))
+        dnp = ctx.enter_context(tc.tile_pool(name="dnp", bufs=3))
+        ilp = ctx.enter_context(tc.tile_pool(name="ilp", bufs=3))
+        trp = ctx.enter_context(tc.tile_pool(name="trp", bufs=4))
+        cwp = ctx.enter_context(tc.tile_pool(name="cwp", bufs=6))
+        cdp = ctx.enter_context(tc.tile_pool(name="cdp", bufs=4))
+        s0p = ctx.enter_context(tc.tile_pool(name="s0p", bufs=3))
+        s1p = ctx.enter_context(tc.tile_pool(name="s1p", bufs=2))
+        tps = ctx.enter_context(tc.psum_pool(name="tps", bufs=4))
+        mmp = ctx.enter_context(tc.psum_pool(name="mmp", bufs=4))
+
+        ident = const.tile([P, P], F32, name="ident")
+        make_identity(nc, ident[:])
+
+        raw = {}
+
+        def loads(px):
+            h, w = divmod(px, 2)
+            zr = zp.tile([P, J, D], F32, name="zt", tag="zt")
+            nc.sync.dma_start(out=zr[:], in_=zv[:, :, 0, h, w, :])
+            gt = gp.tile([P, J, 2, D], BF16, name="gt", tag="gt")
+            nc.sync.dma_start(out=gt[:], in_=gv[:, :, :, h, w, :])
+            wts = []
+            for ri in range(2):
+                wt = wp.tile([P, W4], BF16, name="wt", tag="wt")
+                nc.sync.dma_start(out=wt[:].rearrange("p (q f) -> p q f", q=J), in_=wv[ri][:, h, w])
+                wts.append(wt)
+            zi = zp.tile([P, J, D], F32, name="zt", tag="zt")
+            nc.sync.dma_start(out=zi[:], in_=zv[:, :, 1, h, w, :])
+            xt = xp.tile([P, J, 2, D], BF16, name="xt", tag="xt")
+            nc.sync.dma_start(out=xt[:], in_=xv[:, :, :, h, w, :])
+            raw[px] = ((zr, zi), gt, wts, xt)
+
+        def quantize(pool, tag, src, fmt):
+            codes = pool.tile([P, D], U32, name=tag + "c", tag=tag + "c", align_bytes=64)
+            scales = pool.tile([P, D], U8, name=tag + "s", tag=tag + "s", align_bytes=64)
+            nc.vector.quantize_mx(out=codes[:].bitcast(fmt), scales=scales[:], in_=src[:])
+            return (codes, scales)
+
+        def turn(src):
+            dst = trp.tile([P, W4], BF16, name="tr", tag="tr", align_bytes=64)
+            words = src[:].bitcast(F32)
+            dwords = dst[:].bitcast(F32)
+            for half in range(2):
+                bank = tps.tile([P, D], F32, name="tp", tag="tp")
+                for gg in range(2):
+                    g = 2 * half + gg
+                    for u in range(2):
+                        k = 2 * gg + u
+                        nc.tensor.transpose(
+                            bank[:, P * k : P * (k + 1)], words[:, 256 * g + u : 256 * (g + 1) : 2], ident[:]
+                        )
+                nc.scalar.copy(
+                    out=dwords[:, D * half : D * (half + 1)].rearrange("m (g r u) -> m g r u", g=2, u=2),
+                    in_=bank[:].rearrange("m (g u r) -> m g r u", g=2, u=2),
+                )
+            return dst
+
+        def interleave(kind, part, src3):
+            dst = ilp.tile([P, W4], BF16, name="il", tag="il", align_bytes=64)
+            o = dst[:].rearrange("p (c j) -> p c j", j=J)
+            i = src3.rearrange("p j c -> p c j")
+            if (kind, part) in SCALAR_INTERLEAVES:
+                nc.scalar.copy(out=o, in_=i)
+            else:
+                nc.vector.tensor_copy(out=o, in_=i)
+            return dst
+
+        def product(acc, terms):
+            n = len(terms)
+            for k in range(n):
+                (lc, ls, lf), (rc, rs, rf) = terms[k]
+                nc.tensor.matmul_mx(
+                    out=acc[:],
+                    lhsT=lc.bitcast(lf),
+                    lhsT_scale=ls,
+                    rhs=rc.bitcast(rf),
+                    rhs_scale=rs,
+                    start=(k == 0),
+                    stop=(k == n - 1),
+                )
+
+        loads(0)
+        loads(1)
+        for px in range(NPX):
+            h, w = divmod(px, 2)
+            zts, gt, wts, xt = raw.pop(px)
+
+            dn = []
+            for part in range(2):
+                d = dnp.tile([P, W4], BF16, name="dn", tag="dn", align_bytes=64)
+                nc.vector.scalar_tensor_tensor(
+                    out=d[:].rearrange("p (j f) -> p j f", j=J),
+                    in0=zts[part][:],
+                    scalar=0.0,
+                    in1=gt[:, :, part, :],
+                    op0=ALU.is_gt,
+                    op1=ALU.mult,
+                )
+                dn.append(d)
+
+            wr_t = turn(wts[0])
+            wi_t = turn(wts[1])
+            wr_q = quantize(cwp, "w", wr_t, E4)
+            wi_q = quantize(cwp, "w", wi_t, E4)
+            wn_t = trp.tile([P, W4], BF16, name="tr", tag="tr", align_bytes=64)
+            nc.vector.tensor_scalar_mul(wn_t[:], wi_t[:], -1.0)
+
+            df_q = []
+            db_q = []
+            for part in range(2):
+                dt_t = turn(dn[part])
+                di_t = interleave("d", part, dn[part][:].rearrange("p (j f) -> p j f", j=J))
+                df_q.append(quantize(cdp, "f", dt_t, E5))
+                db_q.append(quantize(cdp, "b", di_t, E5))
+            wn_q = quantize(cwp, "w", wn_t, E4)
+
+            x_q = []
+            xi_t = [interleave("x", part, xt[:, :, part, :]) for part in range(2)]
+            for part in range(2):
+                x_q.append(quantize(cdp, "x", xi_t[part], E4))
+
+            for part in range(2):
+                st = s0p.tile([P, J, D], F32, name="st0", tag="st0")
+                if part == 0:
+                    plan = ((df_q[0], wr_q), (df_q[1], wi_q))
+                else:
+                    plan = ((df_q[1], wr_q), (df_q[0], wn_q))
+                for j in range(J):
+                    acc = mmp.tile([P, D], F32, name="acc", tag="acc")
+                    product(
+                        acc,
+                        [
+                            (
+                                (dq[0][:, P * j : P * (j + 1)], dq[1][:, P * j : P * (j + 1)], E5),
+                                (wq[0][:], wq[1][:], E4),
+                            )
+                            for (dq, wq) in plan
+                        ],
+                    )
+                    nc.scalar.copy(
+                        out=st[:, j, :].rearrange("b (m q) -> b m q", q=J),
+                        in_=acc[:].rearrange("b (q m) -> b m q", q=J),
+                    )
+                nc.scalar.dma_start(out=o0v[:, :, part, h, w, :], in_=st[:])
+
+            st = s1p.tile([P, J, D], F32, name="st1", tag="st1")
+            for t in range(J):
+                acc = mmp.tile([P, D], F32, name="acc", tag="acc")
+                product(
+                    acc,
+                    [
+                        (
+                            (x_q[part][0][:, P * t : P * (t + 1)], x_q[part][1][:, P * t : P * (t + 1)], E4),
+                            (db_q[part][0][:], db_q[part][1][:], E5),
+                        )
+                        for part in range(2)
+                    ],
+                )
+                nc.scalar.copy(out=st[:, t, :], in_=acc[:])
+            nc.scalar.dma_start(out=o1v[:, h, w], in_=st[:])
+
+            if px + 2 < NPX:
+                loads(px + 2)

@@ -19,8 +19,6 @@ W4 = J * D
 
 FLOPS = 6 * NPX * 2 * D * D * D
 
-SCALAR_INTERLEAVES = (("x", 1),)
-
 
 def tile_dot_pa_v_kernel(tc, x_crop, W_r, W_i, b_r, b_i, z, grad_out, out_0, out_1):
     nc = tc.nc
@@ -49,157 +47,196 @@ def tile_dot_pa_v_kernel(tc, x_crop, W_r, W_i, b_r, b_i, z, grad_out, out_0, out
         s1p = ctx.enter_context(tc.tile_pool(name="s1p", bufs=2))
         tps = ctx.enter_context(tc.psum_pool(name="tps", bufs=4))
         mmp = ctx.enter_context(tc.psum_pool(name="mmp", bufs=4))
+        ctx.enter_context(tc.manual_schedule())
 
         ident = const.tile([P, P], F32, name="ident")
         make_identity(nc, ident[:])
 
-        raw = {}
+        r = {}
 
-        def loads(px):
-            h, w = divmod(px, 2)
-            zr = zp.tile([P, J, D], F32, name="zt", tag="zt")
-            nc.sync.dma_start(out=zr[:], in_=zv[:, :, 0, h, w, :])
-            gt = gp.tile([P, J, 2, D], BF16, name="gt", tag="gt")
-            nc.sync.dma_start(out=gt[:], in_=gv[:, :, :, h, w, :])
-            wts = []
-            for ri in range(2):
-                wt = wp.tile([P, W4], BF16, name="wt", tag="wt")
-                nc.sync.dma_start(out=wt[:].rearrange("p (q f) -> p q f", q=J), in_=wv[ri][:, h, w])
-                wts.append(wt)
-            zi = zp.tile([P, J, D], F32, name="zt", tag="zt")
-            nc.sync.dma_start(out=zi[:], in_=zv[:, :, 1, h, w, :])
-            xt = xp.tile([P, J, 2, D], BF16, name="xt", tag="xt")
-            nc.sync.dma_start(out=xt[:], in_=xv[:, :, :, h, w, :])
-            raw[px] = ((zr, zi), gt, wts, xt)
+        def hw(k):
+            return divmod(k, 2)
 
-        def quantize(pool, tag, src, fmt):
-            codes = pool.tile([P, D], U32, name=tag + "c", tag=tag + "c", align_bytes=64)
-            scales = pool.tile([P, D], U8, name=tag + "s", tag=tag + "s", align_bytes=64)
-            nc.vector.quantize_mx(out=codes[:].bitcast(fmt), scales=scales[:], in_=src[:])
-            return (codes, scales)
+        def load_z(k, part):
+            h, w = hw(k)
+            t = zp.tile([P, J, D], F32, name="zt", tag="zt")
+            nc.sync.dma_start(out=t[:], in_=zv[:, :, part, h, w, :])
+            r[("z", k, part)] = t
 
-        def turn(src):
-            dst = trp.tile([P, W4], BF16, name="tr", tag="tr", align_bytes=64)
-            words = src[:].bitcast(F32)
-            dwords = dst[:].bitcast(F32)
+        def load_g(k):
+            h, w = hw(k)
+            t = gp.tile([P, J, 2, D], BF16, name="gt", tag="gt")
+            nc.sync.dma_start(out=t[:], in_=gv[:, :, :, h, w, :])
+            r[("g", k)] = t
+
+        def load_x(k):
+            h, w = hw(k)
+            t = xp.tile([P, J, 2, D], BF16, name="xt", tag="xt")
+            nc.sync.dma_start(out=t[:], in_=xv[:, :, :, h, w, :])
+            r[("x", k)] = t
+
+        def load_w(k, ri):
+            h, w = hw(k)
+            t = wp.tile([P, W4], BF16, name="wt", tag="wt")
+            nc.sync.dma_start(out=t[:].rearrange("p (q f) -> p q f", q=J), in_=wv[ri][:, h, w])
+            r[("w", k, ri)] = t
+
+        def dz(k, part):
+            t = dnp.tile([P, W4], BF16, name="dn", tag="dn", align_bytes=64)
+            nc.vector.scalar_tensor_tensor(
+                out=t[:].rearrange("p (j f) -> p j f", j=J),
+                in0=r[("z", k, part)][:],
+                scalar=0.0,
+                in1=r[("g", k)][:, :, part, :],
+                op0=ALU.is_gt,
+                op1=ALU.mult,
+            )
+            r[("dn", k, part)] = t
+
+        def copy(eng, out, in_):
+            if eng == "V":
+                nc.vector.tensor_copy(out=out, in_=in_)
+            else:
+                nc.scalar.copy(out=out, in_=in_)
+
+        def turn(src, dst, engs="SS"):
+            s = r[src]
+            t = trp.tile([P, W4], BF16, name="tr", tag="tr", align_bytes=64)
+            words = s[:].bitcast(F32)
+            dwords = t[:].bitcast(F32)
             for half in range(2):
                 bank = tps.tile([P, D], F32, name="tp", tag="tp")
                 for gg in range(2):
                     g = 2 * half + gg
                     for u in range(2):
-                        k = 2 * gg + u
+                        c = 2 * gg + u
                         nc.tensor.transpose(
-                            bank[:, P * k : P * (k + 1)], words[:, 256 * g + u : 256 * (g + 1) : 2], ident[:]
+                            bank[:, P * c : P * (c + 1)], words[:, 256 * g + u : 256 * (g + 1) : 2], ident[:]
                         )
-                nc.scalar.copy(
-                    out=dwords[:, D * half : D * (half + 1)].rearrange("m (g r u) -> m g r u", g=2, u=2),
-                    in_=bank[:].rearrange("m (g u r) -> m g r u", g=2, u=2),
+                copy(
+                    engs[half],
+                    dwords[:, D * half : D * (half + 1)].rearrange("m (g r u) -> m g r u", g=2, u=2),
+                    bank[:].rearrange("m (g u r) -> m g r u", g=2, u=2),
                 )
-            return dst
+            r[dst] = t
 
-        def interleave(kind, part, src3):
-            dst = ilp.tile([P, W4], BF16, name="il", tag="il", align_bytes=64)
-            o = dst[:].rearrange("p (c j) -> p c j", j=J)
-            i = src3.rearrange("p j c -> p c j")
-            if (kind, part) in SCALAR_INTERLEAVES:
-                nc.scalar.copy(out=o, in_=i)
+        def quant(src, dst, fmt):
+            pool = cwp if dst[0] == "qw" else cdp
+            tag = dst[0]
+            codes = pool.tile([P, D], U32, name=tag + "c", tag=tag + "c", align_bytes=64)
+            scales = pool.tile([P, D], U8, name=tag + "s", tag=tag + "s", align_bytes=64)
+            nc.vector.quantize_mx(out=codes[:].bitcast(fmt), scales=scales[:], in_=r[src][:])
+            r[dst] = (codes, scales)
+
+        def negate(k):
+            t = trp.tile([P, W4], BF16, name="tr", tag="tr", align_bytes=64)
+            nc.vector.tensor_scalar_mul(t[:], r[("wt", k, 1)][:], -1.0)
+            r[("wt", k, 2)] = t
+
+        def inter(eng, src3, dst):
+            t = ilp.tile([P, W4], BF16, name="il", tag="il", align_bytes=64)
+            copy(eng, t[:].rearrange("p (c j) -> p c j", j=J), src3.rearrange("p j c -> p c j"))
+            r[dst] = t
+
+        def inter_d(eng, k, part):
+            inter(eng, r[("dn", k, part)][:].rearrange("p (j f) -> p j f", j=J), ("di", k, part))
+
+        def inter_x(eng, k, part):
+            inter(eng, r[("x", k)][:, :, part, :], ("xi", k, part))
+
+        def mx(acc, lq, lo, lf, rq, rf, start, stop):
+            nc.tensor.matmul_mx(
+                out=acc[:],
+                lhsT=lq[0][:, lo : lo + P].bitcast(lf),
+                lhsT_scale=lq[1][:, lo : lo + P],
+                rhs=rq[0][:].bitcast(rf),
+                rhs_scale=rq[1][:],
+                start=start,
+                stop=stop,
+            )
+
+        def m0(k, part, engs="SSSS", queue="S"):
+            h, w = hw(k)
+            st = s0p.tile([P, J, D], F32, name="st0", tag="st0")
+            if part == 0:
+                plan = ((0, 0), (1, 1))
             else:
-                nc.vector.tensor_copy(out=o, in_=i)
-            return dst
-
-        def product(acc, terms):
-            n = len(terms)
-            for k in range(n):
-                (lc, ls, lf), (rc, rs, rf) = terms[k]
-                nc.tensor.matmul_mx(
-                    out=acc[:],
-                    lhsT=lc.bitcast(lf),
-                    lhsT_scale=ls,
-                    rhs=rc.bitcast(rf),
-                    rhs_scale=rs,
-                    start=(k == 0),
-                    stop=(k == n - 1),
+                plan = ((1, 0), (0, 2))
+            for j in range(J):
+                acc = mmp.tile([P, D], F32, name="acc", tag="acc")
+                for n in range(2):
+                    dpart, wkind = plan[n]
+                    mx(acc, r[("qf", k, dpart)], P * j, E5, r[("qw", k, wkind)], E4, n == 0, n == 1)
+                copy(
+                    engs[j],
+                    st[:, j, :].rearrange("b (m q) -> b m q", q=J),
+                    acc[:].rearrange("b (q m) -> b m q", q=J),
                 )
+            store(queue, o0v[:, :, part, h, w, :], st[:])
 
-        loads(0)
-        loads(1)
-        for px in range(NPX):
-            h, w = divmod(px, 2)
-            zts, gt, wts, xt = raw.pop(px)
+        def store(queue, out, in_):
+            if queue == "S":
+                nc.scalar.dma_start(out=out, in_=in_)
+            else:
+                nc.sync.dma_start(out=out, in_=in_)
 
-            dn = []
-            for part in range(2):
-                d = dnp.tile([P, W4], BF16, name="dn", tag="dn", align_bytes=64)
-                nc.vector.scalar_tensor_tensor(
-                    out=d[:].rearrange("p (j f) -> p j f", j=J),
-                    in0=zts[part][:],
-                    scalar=0.0,
-                    in1=gt[:, :, part, :],
-                    op0=ALU.is_gt,
-                    op1=ALU.mult,
-                )
-                dn.append(d)
-
-            wr_t = turn(wts[0])
-            wi_t = turn(wts[1])
-            wr_q = quantize(cwp, "w", wr_t, E4)
-            wi_q = quantize(cwp, "w", wi_t, E4)
-            wn_t = trp.tile([P, W4], BF16, name="tr", tag="tr", align_bytes=64)
-            nc.vector.tensor_scalar_mul(wn_t[:], wi_t[:], -1.0)
-
-            df_q = []
-            db_q = []
-            for part in range(2):
-                dt_t = turn(dn[part])
-                di_t = interleave("d", part, dn[part][:].rearrange("p (j f) -> p j f", j=J))
-                df_q.append(quantize(cdp, "f", dt_t, E5))
-                db_q.append(quantize(cdp, "b", di_t, E5))
-            wn_q = quantize(cwp, "w", wn_t, E4)
-
-            x_q = []
-            xi_t = [interleave("x", part, xt[:, :, part, :]) for part in range(2)]
-            for part in range(2):
-                x_q.append(quantize(cdp, "x", xi_t[part], E4))
-
-            for part in range(2):
-                st = s0p.tile([P, J, D], F32, name="st0", tag="st0")
-                if part == 0:
-                    plan = ((df_q[0], wr_q), (df_q[1], wi_q))
-                else:
-                    plan = ((df_q[1], wr_q), (df_q[0], wn_q))
-                for j in range(J):
-                    acc = mmp.tile([P, D], F32, name="acc", tag="acc")
-                    product(
-                        acc,
-                        [
-                            (
-                                (dq[0][:, P * j : P * (j + 1)], dq[1][:, P * j : P * (j + 1)], E5),
-                                (wq[0][:], wq[1][:], E4),
-                            )
-                            for (dq, wq) in plan
-                        ],
-                    )
-                    nc.scalar.copy(
-                        out=st[:, j, :].rearrange("b (m q) -> b m q", q=J),
-                        in_=acc[:].rearrange("b (q m) -> b m q", q=J),
-                    )
-                nc.scalar.dma_start(out=o0v[:, :, part, h, w, :], in_=st[:])
-
+        def m1(k, engs="SSSS", queue="S"):
+            h, w = hw(k)
             st = s1p.tile([P, J, D], F32, name="st1", tag="st1")
             for t in range(J):
                 acc = mmp.tile([P, D], F32, name="acc", tag="acc")
-                product(
-                    acc,
-                    [
-                        (
-                            (x_q[part][0][:, P * t : P * (t + 1)], x_q[part][1][:, P * t : P * (t + 1)], E4),
-                            (db_q[part][0][:], db_q[part][1][:], E5),
-                        )
-                        for part in range(2)
-                    ],
-                )
-                nc.scalar.copy(out=st[:, t, :], in_=acc[:])
-            nc.scalar.dma_start(out=o1v[:, h, w], in_=st[:])
+                for part in range(2):
+                    mx(acc, r[("qx", k, part)], P * t, E4, r[("qb", k, part)], E5, part == 0, part == 1)
+                copy(engs[t], st[:, t, :], acc[:])
+            store(queue, o1v[:, h, w], st[:])
 
-            if px + 2 < NPX:
-                loads(px + 2)
+        def loads(k):
+            if k == 0:
+                load_z(k, 0)
+                load_g(k)
+                load_z(k, 1)
+                load_w(k, 0)
+                load_w(k, 1)
+            else:
+                load_w(k, 0)
+                load_w(k, 1)
+                load_z(k, 0)
+                load_g(k)
+                load_z(k, 1)
+            load_x(k)
+
+        loads(0)
+        loads(1)
+        for k in range(NPX):
+            dz(k, 0)
+            if k > 0:
+                m1(k - 1)
+            turn(("dn", k, 0), ("dt", k, 0))
+            dz(k, 1)
+            if k == 0:
+                turn(("w", 0, 0), ("wt", 0, 0))
+                turn(("w", 0, 1), ("wt", 0, 1))
+            turn(("dn", k, 1), ("dt", k, 1))
+            quant(("wt", k, 0), ("qw", k, 0), E4)
+            quant(("wt", k, 1), ("qw", k, 1), E4)
+            negate(k)
+            inter_x("S", k, 1)
+            inter_d("V", k, 0)
+            quant(("dt", k, 0), ("qf", k, 0), E5)
+            quant(("wt", k, 2), ("qw", k, 2), E4)
+            if k + 1 < NPX:
+                turn(("w", k + 1, 0), ("wt", k + 1, 0))
+            inter_d("V", k, 1)
+            quant(("dt", k, 1), ("qf", k, 1), E5)
+            quant(("di", k, 0), ("qb", k, 0), E5)
+            if k + 1 < NPX:
+                turn(("w", k + 1, 1), ("wt", k + 1, 1))
+            inter_x("V", k, 0)
+            quant(("di", k, 1), ("qb", k, 1), E5)
+            m0(k, 0)
+            quant(("xi", k, 1), ("qx", k, 1), E4)
+            quant(("xi", k, 0), ("qx", k, 0), E4)
+            m0(k, 1)
+            if k + 2 < NPX:
+                loads(k + 2)
+        m1(NPX - 1)

@@ -14,22 +14,21 @@ ALU = mybir.AluOpType
 P = 128
 J = 4
 D = 512
-NPX = 4
 W4 = J * D
 
-FLOPS = 6 * NPX * 2 * D * D * D
+FLOPS = 6 * 4 * 2 * D * D * D
 
 
 def tile_dot_pa_v_kernel(tc, x_crop, W_r, W_i, b_r, b_i, z, grad_out, out_0, out_1):
     nc = tc.nc
-    xv = x_crop.rearrange("(p j) r h w c -> p j r h w c", j=J)
-    gv = grad_out.rearrange("(p j) r h w f -> p j r h w f", j=J)
-    zv = z.rearrange("(p j) r h w f -> p j r h w f", j=J)
+    xv = x_crop.rearrange("(p j) r h w c -> p j r h (w c)", j=J)
+    gv = grad_out.rearrange("(p j) r h w f -> p j r h (w f)", j=J)
+    zv = z.rearrange("(p j) r h w f -> p j r h (w f)", j=J)
     wv = (
-        W_r.rearrange("h w (p q) f -> p h w q f", q=J),
-        W_i.rearrange("h w (p q) f -> p h w q f", q=J),
+        W_r.rearrange("h w (p q) f -> p h w (q f)", q=J),
+        W_i.rearrange("h w (p q) f -> p h w (q f)", q=J),
     )
-    o0v = out_0.rearrange("(p j) r h w c -> p j r h w c", j=J)
+    o0v = out_0.rearrange("(p j) r h w c -> p j r h (w c)", j=J)
     o1v = out_1.rearrange("h w (t m) f -> m h w t f", t=J)
 
     with ExitStack() as ctx:
@@ -37,13 +36,13 @@ def tile_dot_pa_v_kernel(tc, x_crop, W_r, W_i, b_r, b_i, z, grad_out, out_0, out
         zp = ctx.enter_context(tc.tile_pool(name="zp", bufs=4))
         gp = ctx.enter_context(tc.tile_pool(name="gp", bufs=2))
         xp = ctx.enter_context(tc.tile_pool(name="xp", bufs=2))
-        wp = ctx.enter_context(tc.tile_pool(name="wp", bufs=4))
+        wp = ctx.enter_context(tc.tile_pool(name="wp", bufs=2))
         dnp = ctx.enter_context(tc.tile_pool(name="dnp", bufs=3))
-        ilp = ctx.enter_context(tc.tile_pool(name="ilp", bufs=3))
+        ilp = ctx.enter_context(tc.tile_pool(name="ilp", bufs=4))
         trp = ctx.enter_context(tc.tile_pool(name="trp", bufs=4))
         cwp = ctx.enter_context(tc.tile_pool(name="cwp", bufs=6))
         cdp = ctx.enter_context(tc.tile_pool(name="cdp", bufs=4))
-        s0p = ctx.enter_context(tc.tile_pool(name="s0p", bufs=3))
+        s0p = ctx.enter_context(tc.tile_pool(name="s0p", bufs=4))
         s1p = ctx.enter_context(tc.tile_pool(name="s1p", bufs=2))
         tps = ctx.enter_context(tc.psum_pool(name="tps", bufs=4))
         mmp = ctx.enter_context(tc.psum_pool(name="mmp", bufs=4))
@@ -54,44 +53,39 @@ def tile_dot_pa_v_kernel(tc, x_crop, W_r, W_i, b_r, b_i, z, grad_out, out_0, out
 
         r = {}
 
-        def hw(k):
-            return divmod(k, 2)
+        def load_z(h, part):
+            for jp in range(2):
+                t = zp.tile([P, 2, 2 * D], F32, name="zt", tag="zt")
+                nc.sync.dma_start(out=t[:], in_=zv[:, 2 * jp : 2 * jp + 2, part, h, :])
+                r[("z", h, part, jp)] = t
 
-        def load_z(k, part):
-            h, w = hw(k)
-            t = zp.tile([P, J, D], F32, name="zt", tag="zt")
-            nc.sync.dma_start(out=t[:], in_=zv[:, :, part, h, w, :])
-            r[("z", k, part)] = t
+        def load_g(h, part):
+            t = gp.tile([P, J, 2 * D], BF16, name="gt", tag="gt")
+            nc.sync.dma_start(out=t[:], in_=gv[:, :, part, h, :])
+            r[("g", h, part)] = t
 
-        def load_g(k):
-            h, w = hw(k)
-            t = gp.tile([P, J, 2, D], BF16, name="gt", tag="gt")
-            nc.sync.dma_start(out=t[:], in_=gv[:, :, :, h, w, :])
-            r[("g", k)] = t
+        def load_x(h, part):
+            t = xp.tile([P, J, 2 * D], BF16, name="xt", tag="xt")
+            nc.sync.dma_start(out=t[:], in_=xv[:, :, part, h, :])
+            r[("x", h, part)] = t
 
-        def load_x(k):
-            h, w = hw(k)
-            t = xp.tile([P, J, 2, D], BF16, name="xt", tag="xt")
-            nc.sync.dma_start(out=t[:], in_=xv[:, :, :, h, w, :])
-            r[("x", k)] = t
+        def load_w(h, ri):
+            t = wp.tile([P, 2, W4], BF16, name="wt", tag="wt")
+            nc.sync.dma_start(out=t[:], in_=wv[ri][:, h])
+            r[("w", h, ri)] = t
 
-        def load_w(k, ri):
-            h, w = hw(k)
-            t = wp.tile([P, W4], BF16, name="wt", tag="wt")
-            nc.sync.dma_start(out=t[:].rearrange("p (q f) -> p q f", q=J), in_=wv[ri][:, h, w])
-            r[("w", k, ri)] = t
-
-        def dz(k, part):
-            t = dnp.tile([P, W4], BF16, name="dn", tag="dn", align_bytes=64)
-            nc.vector.scalar_tensor_tensor(
-                out=t[:].rearrange("p (j f) -> p j f", j=J),
-                in0=r[("z", k, part)][:],
-                scalar=0.0,
-                in1=r[("g", k)][:, :, part, :],
-                op0=ALU.is_gt,
-                op1=ALU.mult,
-            )
-            r[("dn", k, part)] = t
+        def dz(h, part):
+            t = dnp.tile([P, J, 2 * D], BF16, name="dn", tag="dn", align_bytes=64)
+            for jp in range(2):
+                nc.vector.scalar_tensor_tensor(
+                    out=t[:, 2 * jp : 2 * jp + 2, :],
+                    in0=r[("z", h, part, jp)][:],
+                    scalar=0.0,
+                    in1=r[("g", h, part)][:, 2 * jp : 2 * jp + 2, :],
+                    op0=ALU.is_gt,
+                    op1=ALU.mult,
+                )
+            r[("dn", h, part)] = t
 
         def copy(eng, out, in_):
             if eng == "V":
@@ -99,26 +93,32 @@ def tile_dot_pa_v_kernel(tc, x_crop, W_r, W_i, b_r, b_i, z, grad_out, out_0, out
             else:
                 nc.scalar.copy(out=out, in_=in_)
 
-        def turn(src, dst, engs="SS"):
-            s = r[src]
+        def turn(words, first, step, dst, engs="SS"):
             t = trp.tile([P, W4], BF16, name="tr", tag="tr", align_bytes=64)
-            words = s[:].bitcast(F32)
             dwords = t[:].bitcast(F32)
             for half in range(2):
                 bank = tps.tile([P, D], F32, name="tp", tag="tp")
                 for gg in range(2):
-                    g = 2 * half + gg
+                    lo = first + (2 * half + gg) * step
                     for u in range(2):
                         c = 2 * gg + u
-                        nc.tensor.transpose(
-                            bank[:, P * c : P * (c + 1)], words[:, 256 * g + u : 256 * (g + 1) : 2], ident[:]
-                        )
+                        nc.tensor.transpose(bank[:, P * c : P * (c + 1)], words[:, lo + u : lo + 256 : 2], ident[:])
                 copy(
                     engs[half],
                     dwords[:, D * half : D * (half + 1)].rearrange("m (g r u) -> m g r u", g=2, u=2),
                     bank[:].rearrange("m (g u r) -> m g r u", g=2, u=2),
                 )
             r[dst] = t
+
+        def turn_d(k, part):
+            h, w = divmod(k, 2)
+            words = r[("dn", h, part)][:].rearrange("p j f -> p (j f)").bitcast(F32)
+            turn(words, 256 * w, 512, ("dt", k, part))
+
+        def turn_w(k, ri):
+            h, w = divmod(k, 2)
+            words = r[("w", h, ri)][:].rearrange("p w f -> p (w f)").bitcast(F32)
+            turn(words, 1024 * w, 256, ("wt", k, ri))
 
         def quant(src, dst, fmt):
             pool = cwp if dst[0] == "qw" else cdp
@@ -133,16 +133,12 @@ def tile_dot_pa_v_kernel(tc, x_crop, W_r, W_i, b_r, b_i, z, grad_out, out_0, out
             nc.vector.tensor_scalar_mul(t[:], r[("wt", k, 1)][:], -1.0)
             r[("wt", k, 2)] = t
 
-        def inter(eng, src3, dst):
+        def inter(eng, kind, k, part):
+            h, w = divmod(k, 2)
+            src3 = r[(kind, h, part)][:, :, D * w : D * (w + 1)]
             t = ilp.tile([P, W4], BF16, name="il", tag="il", align_bytes=64)
             copy(eng, t[:].rearrange("p (c j) -> p c j", j=J), src3.rearrange("p j c -> p c j"))
-            r[dst] = t
-
-        def inter_d(eng, k, part):
-            inter(eng, r[("dn", k, part)][:].rearrange("p (j f) -> p j f", j=J), ("di", k, part))
-
-        def inter_x(eng, k, part):
-            inter(eng, r[("x", k)][:, :, part, :], ("xi", k, part))
+            r[(kind + "i", k, part)] = t
 
         def mx(acc, lq, lo, lf, rq, rf, start, stop):
             nc.tensor.matmul_mx(
@@ -155,88 +151,118 @@ def tile_dot_pa_v_kernel(tc, x_crop, W_r, W_i, b_r, b_i, z, grad_out, out_0, out
                 stop=stop,
             )
 
-        def m0(k, part, engs="SSSS", queue="S"):
-            h, w = hw(k)
-            st = s0p.tile([P, J, D], F32, name="st0", tag="st0")
+        def m0(h, part, jp, engs="SSSS"):
+            st = s0p.tile([P, 2, 2, D], F32, name="st0", tag="st0")
             if part == 0:
                 plan = ((0, 0), (1, 1))
             else:
                 plan = ((1, 0), (0, 2))
-            for j in range(J):
-                acc = mmp.tile([P, D], F32, name="acc", tag="acc")
-                for n in range(2):
-                    dpart, wkind = plan[n]
-                    mx(acc, r[("qf", k, dpart)], P * j, E5, r[("qw", k, wkind)], E4, n == 0, n == 1)
-                copy(
-                    engs[j],
-                    st[:, j, :].rearrange("b (m q) -> b m q", q=J),
-                    acc[:].rearrange("b (q m) -> b m q", q=J),
-                )
-            store(queue, o0v[:, :, part, h, w, :], st[:])
+            for jj in range(2):
+                for w in range(2):
+                    k = 2 * h + w
+                    acc = mmp.tile([P, D], F32, name="acc", tag="acc")
+                    for n in range(2):
+                        dpart, wkind = plan[n]
+                        mx(acc, r[("qf", k, dpart)], P * (2 * jp + jj), E5, r[("qw", k, wkind)], E4, n == 0, n == 1)
+                    copy(
+                        engs[2 * jj + w],
+                        st[:, jj, w, :].rearrange("b (m q) -> b m q", q=J),
+                        acc[:].rearrange("b (q m) -> b m q", q=J),
+                    )
+            nc.scalar.dma_start(
+                out=o0v[:, 2 * jp : 2 * jp + 2, part, h, :], in_=st[:].rearrange("b j w c -> b j (w c)")
+            )
 
-        def store(queue, out, in_):
-            if queue == "S":
-                nc.scalar.dma_start(out=out, in_=in_)
-            else:
-                nc.sync.dma_start(out=out, in_=in_)
-
-        def m1(k, engs="SSSS", queue="S"):
-            h, w = hw(k)
+        def m1(k, engs="SSSS"):
+            h, w = divmod(k, 2)
             st = s1p.tile([P, J, D], F32, name="st1", tag="st1")
             for t in range(J):
                 acc = mmp.tile([P, D], F32, name="acc", tag="acc")
                 for part in range(2):
                     mx(acc, r[("qx", k, part)], P * t, E4, r[("qb", k, part)], E5, part == 0, part == 1)
                 copy(engs[t], st[:, t, :], acc[:])
-            store(queue, o1v[:, h, w], st[:])
+            nc.scalar.dma_start(out=o1v[:, h, w], in_=st[:])
 
-        def loads(k):
-            if k == 0:
-                load_z(k, 0)
-                load_g(k)
-                load_z(k, 1)
-                load_w(k, 0)
-                load_w(k, 1)
-            else:
-                load_w(k, 0)
-                load_w(k, 1)
-                load_z(k, 0)
-                load_g(k)
-                load_z(k, 1)
-            load_x(k)
+        def q_f(k, part):
+            quant(("dt", k, part), ("qf", k, part), E5)
 
-        loads(0)
-        loads(1)
-        for k in range(NPX):
-            dz(k, 0)
-            if k > 0:
-                m1(k - 1)
-            turn(("dn", k, 0), ("dt", k, 0))
-            dz(k, 1)
-            if k == 0:
-                turn(("w", 0, 0), ("wt", 0, 0))
-                turn(("w", 0, 1), ("wt", 0, 1))
-            turn(("dn", k, 1), ("dt", k, 1))
-            quant(("wt", k, 0), ("qw", k, 0), E4)
-            quant(("wt", k, 1), ("qw", k, 1), E4)
-            negate(k)
-            inter_x("S", k, 1)
-            inter_d("V", k, 0)
-            quant(("dt", k, 0), ("qf", k, 0), E5)
-            quant(("wt", k, 2), ("qw", k, 2), E4)
-            if k + 1 < NPX:
-                turn(("w", k + 1, 0), ("wt", k + 1, 0))
-            inter_d("V", k, 1)
-            quant(("dt", k, 1), ("qf", k, 1), E5)
-            quant(("di", k, 0), ("qb", k, 0), E5)
-            if k + 1 < NPX:
-                turn(("w", k + 1, 1), ("wt", k + 1, 1))
-            inter_x("V", k, 0)
-            quant(("di", k, 1), ("qb", k, 1), E5)
-            m0(k, 0)
-            quant(("xi", k, 1), ("qx", k, 1), E4)
-            quant(("xi", k, 0), ("qx", k, 0), E4)
-            m0(k, 1)
-            if k + 2 < NPX:
-                loads(k + 2)
-        m1(NPX - 1)
+        def q_b(k, part):
+            quant(("dni", k, part), ("qb", k, part), E5)
+
+        def q_x(k, part):
+            quant(("xi", k, part), ("qx", k, part), E4)
+
+        def q_w(h):
+            for k in (2 * h, 2 * h + 1):
+                quant(("wt", k, 0), ("qw", k, 0), E4)
+                quant(("wt", k, 1), ("qw", k, 1), E4)
+                negate(k)
+            for k in (2 * h, 2 * h + 1):
+                quant(("wt", k, 2), ("qw", k, 2), E4)
+
+        def load_zg(h):
+            for part in range(2):
+                load_g(h, part)
+                load_z(h, part)
+
+        load_zg(0)
+        load_w(0, 0)
+        load_w(0, 1)
+        load_x(0, 0)
+        load_x(0, 1)
+        for h in range(2):
+            a = 2 * h
+            b = a + 1
+            dz(h, 0)
+            if h == 1:
+                m1(0)
+                q_w(1)
+            turn_d(a, 0)
+            turn_d(b, 0)
+            if h == 0:
+                inter("V", "dn", a, 0)
+                inter("V", "dn", b, 0)
+            dz(h, 1)
+            if h == 1:
+                m1(1)
+            turn_d(a, 1)
+            turn_d(b, 1)
+            if h == 0:
+                q_b(a, 0)
+                q_b(b, 0)
+            q_f(a, 0)
+            q_f(b, 0)
+            if h == 0:
+                turn_w(a, 0)
+                turn_w(b, 0)
+            q_f(a, 1)
+            q_f(b, 1)
+            if h == 0:
+                turn_w(a, 1)
+                turn_w(b, 1)
+                load_w(1, 0)
+                load_w(1, 1)
+                load_zg(1)
+                q_w(0)
+            inter("S", "x", a, 1)
+            inter("S", "x", b, 1)
+            for k in (a, b):
+                m0(h, k - a, 0)
+                if h == 1:
+                    inter("V", "dn", k, 0)
+                inter("V", "dn", k, 1)
+                if h == 1:
+                    q_b(k, 0)
+                q_b(k, 1)
+                m0(h, k - a, 1)
+                inter("V", "x", k, 0)
+                q_x(k, 1)
+                q_x(k, 0)
+            if h == 0:
+                load_x(1, 0)
+                load_x(1, 1)
+                for ri in range(2):
+                    turn_w(2, ri)
+                    turn_w(3, ri)
+        m1(2, "SVSV")
+        m1(3, "SVSV")

@@ -14,21 +14,22 @@ ALU = mybir.AluOpType
 P = 128
 J = 4
 D = 512
+NPX = 4
 W4 = J * D
 
-FLOPS = 6 * 4 * 2 * D * D * D
+FLOPS = 6 * NPX * 2 * D * D * D
 
 
 def tile_dot_pa_v_kernel(tc, x_crop, W_r, W_i, b_r, b_i, z, grad_out, out_0, out_1):
     nc = tc.nc
-    xv = x_crop.rearrange("(p j) r h w c -> p j r h (w c)", j=J)
-    gv = grad_out.rearrange("(p j) r h w f -> p j r h (w f)", j=J)
-    zv = z.rearrange("(p j) r h w f -> p j r h (w f)", j=J)
+    xv = x_crop.rearrange("(p j) r h w c -> p j r h w c", j=J)
+    gv = grad_out.rearrange("(p j) r h w f -> p j r h w f", j=J)
+    zv = z.rearrange("(p j) r h w f -> p j r h w f", j=J)
     wv = (
-        W_r.rearrange("h w (p q) f -> p h w (q f)", q=J),
-        W_i.rearrange("h w (p q) f -> p h w (q f)", q=J),
+        W_r.rearrange("h w (p q) f -> p h w q f", q=J),
+        W_i.rearrange("h w (p q) f -> p h w q f", q=J),
     )
-    o0v = out_0.rearrange("(p j) r h w c -> p j r h (w c)", j=J)
+    o0v = out_0.rearrange("(p j) r h w c -> p j r h w c", j=J)
     o1v = out_1.rearrange("h w (t m) f -> m h w t f", t=J)
 
     with ExitStack() as ctx:
@@ -36,14 +37,14 @@ def tile_dot_pa_v_kernel(tc, x_crop, W_r, W_i, b_r, b_i, z, grad_out, out_0, out
         zp = ctx.enter_context(tc.tile_pool(name="zp", bufs=4))
         gp = ctx.enter_context(tc.tile_pool(name="gp", bufs=2))
         xp = ctx.enter_context(tc.tile_pool(name="xp", bufs=2))
-        wp = ctx.enter_context(tc.tile_pool(name="wp", bufs=2))
+        wp = ctx.enter_context(tc.tile_pool(name="wp", bufs=4))
         dnp = ctx.enter_context(tc.tile_pool(name="dnp", bufs=3))
-        ilp = ctx.enter_context(tc.tile_pool(name="ilp", bufs=4))
+        ilp = ctx.enter_context(tc.tile_pool(name="ilp", bufs=3))
         trp = ctx.enter_context(tc.tile_pool(name="trp", bufs=4))
         cwp = ctx.enter_context(tc.tile_pool(name="cwp", bufs=6))
         cdp = ctx.enter_context(tc.tile_pool(name="cdp", bufs=4))
-        s0p = ctx.enter_context(tc.tile_pool(name="s0p", bufs=4))
-        s1p = ctx.enter_context(tc.tile_pool(name="s1p", bufs=2))
+        s0p = ctx.enter_context(tc.tile_pool(name="s0p", bufs=3))
+        s1p = ctx.enter_context(tc.tile_pool(name="s1p", bufs=4))
         tps = ctx.enter_context(tc.psum_pool(name="tps", bufs=4))
         mmp = ctx.enter_context(tc.psum_pool(name="mmp", bufs=4))
         ctx.enter_context(tc.manual_schedule())
@@ -53,39 +54,44 @@ def tile_dot_pa_v_kernel(tc, x_crop, W_r, W_i, b_r, b_i, z, grad_out, out_0, out
 
         r = {}
 
-        def load_z(h, part):
-            for jp in range(2):
-                t = zp.tile([P, 2, 2 * D], F32, name="zt", tag="zt")
-                nc.sync.dma_start(out=t[:], in_=zv[:, 2 * jp : 2 * jp + 2, part, h, :])
-                r[("z", h, part, jp)] = t
+        def hw(k):
+            return divmod(k, 2)
 
-        def load_g(h, part):
-            t = gp.tile([P, J, 2 * D], BF16, name="gt", tag="gt")
-            nc.sync.dma_start(out=t[:], in_=gv[:, :, part, h, :])
-            r[("g", h, part)] = t
+        def load_z(k, part):
+            h, w = hw(k)
+            t = zp.tile([P, J, D], F32, name="zt", tag="zt")
+            nc.sync.dma_start(out=t[:], in_=zv[:, :, part, h, w, :])
+            r[("z", k, part)] = t
 
-        def load_x(h, part):
-            t = xp.tile([P, J, 2 * D], BF16, name="xt", tag="xt")
-            nc.sync.dma_start(out=t[:], in_=xv[:, :, part, h, :])
-            r[("x", h, part)] = t
+        def load_g(k):
+            h, w = hw(k)
+            t = gp.tile([P, J, 2, D], BF16, name="gt", tag="gt")
+            nc.sync.dma_start(out=t[:], in_=gv[:, :, :, h, w, :])
+            r[("g", k)] = t
 
-        def load_w(h, ri):
-            t = wp.tile([P, 2, W4], BF16, name="wt", tag="wt")
-            nc.sync.dma_start(out=t[:], in_=wv[ri][:, h])
-            r[("w", h, ri)] = t
+        def load_x(k):
+            h, w = hw(k)
+            t = xp.tile([P, J, 2, D], BF16, name="xt", tag="xt")
+            nc.sync.dma_start(out=t[:], in_=xv[:, :, :, h, w, :])
+            r[("x", k)] = t
 
-        def dz(h, part):
-            t = dnp.tile([P, J, 2 * D], BF16, name="dn", tag="dn", align_bytes=64)
-            for jp in range(2):
-                nc.vector.scalar_tensor_tensor(
-                    out=t[:, 2 * jp : 2 * jp + 2, :],
-                    in0=r[("z", h, part, jp)][:],
-                    scalar=0.0,
-                    in1=r[("g", h, part)][:, 2 * jp : 2 * jp + 2, :],
-                    op0=ALU.is_gt,
-                    op1=ALU.mult,
-                )
-            r[("dn", h, part)] = t
+        def load_w(k, ri):
+            h, w = hw(k)
+            t = wp.tile([P, W4], BF16, name="wt", tag="wt")
+            nc.sync.dma_start(out=t[:].rearrange("p (q f) -> p q f", q=J), in_=wv[ri][:, h, w])
+            r[("w", k, ri)] = t
+
+        def dz(k, part):
+            t = dnp.tile([P, W4], BF16, name="dn", tag="dn", align_bytes=64)
+            nc.vector.scalar_tensor_tensor(
+                out=t[:].rearrange("p (j f) -> p j f", j=J),
+                in0=r[("z", k, part)][:],
+                scalar=0.0,
+                in1=r[("g", k)][:, :, part, :],
+                op0=ALU.is_gt,
+                op1=ALU.mult,
+            )
+            r[("dn", k, part)] = t
 
         def copy(eng, out, in_):
             if eng == "V":
@@ -93,32 +99,26 @@ def tile_dot_pa_v_kernel(tc, x_crop, W_r, W_i, b_r, b_i, z, grad_out, out_0, out
             else:
                 nc.scalar.copy(out=out, in_=in_)
 
-        def turn(words, first, step, dst, engs="SS"):
+        def turn(src, dst, engs="SS"):
+            s = r[src]
             t = trp.tile([P, W4], BF16, name="tr", tag="tr", align_bytes=64)
+            words = s[:].bitcast(F32)
             dwords = t[:].bitcast(F32)
             for half in range(2):
                 bank = tps.tile([P, D], F32, name="tp", tag="tp")
                 for gg in range(2):
-                    lo = first + (2 * half + gg) * step
+                    g = 2 * half + gg
                     for u in range(2):
                         c = 2 * gg + u
-                        nc.tensor.transpose(bank[:, P * c : P * (c + 1)], words[:, lo + u : lo + 256 : 2], ident[:])
+                        nc.tensor.transpose(
+                            bank[:, P * c : P * (c + 1)], words[:, 256 * g + u : 256 * (g + 1) : 2], ident[:]
+                        )
                 copy(
                     engs[half],
                     dwords[:, D * half : D * (half + 1)].rearrange("m (g r u) -> m g r u", g=2, u=2),
                     bank[:].rearrange("m (g u r) -> m g r u", g=2, u=2),
                 )
             r[dst] = t
-
-        def turn_d(k, part):
-            h, w = divmod(k, 2)
-            words = r[("dn", h, part)][:].rearrange("p j f -> p (j f)").bitcast(F32)
-            turn(words, 256 * w, 512, ("dt", k, part))
-
-        def turn_w(k, ri):
-            h, w = divmod(k, 2)
-            words = r[("w", h, ri)][:].rearrange("p w f -> p (w f)").bitcast(F32)
-            turn(words, 1024 * w, 256, ("wt", k, ri))
 
         def quant(src, dst, fmt):
             pool = cwp if dst[0] == "qw" else cdp
@@ -133,12 +133,16 @@ def tile_dot_pa_v_kernel(tc, x_crop, W_r, W_i, b_r, b_i, z, grad_out, out_0, out
             nc.vector.tensor_scalar_mul(t[:], r[("wt", k, 1)][:], -1.0)
             r[("wt", k, 2)] = t
 
-        def inter(eng, kind, k, part):
-            h, w = divmod(k, 2)
-            src3 = r[(kind, h, part)][:, :, D * w : D * (w + 1)]
+        def inter(eng, src3, dst):
             t = ilp.tile([P, W4], BF16, name="il", tag="il", align_bytes=64)
-            copy(eng, t[:].rearrange("p (c j) -> p c j", j=J), src3.rearrange("p j c -> p c j"))
-            r[(kind + "i", k, part)] = t
+            copy(eng, t[:].rearrange("p (c i j) -> p c j i", i=4, j=J), src3.rearrange("p j (c i) -> p c j i", i=4))
+            r[dst] = t
+
+        def inter_d(eng, k, part):
+            inter(eng, r[("dn", k, part)][:].rearrange("p (j f) -> p j f", j=J), ("di", k, part))
+
+        def inter_x(eng, k, part):
+            inter(eng, r[("x", k)][:, :, part, :], ("xi", k, part))
 
         def mx(acc, lq, lo, lf, rq, rf, start, stop):
             nc.tensor.matmul_mx(
@@ -151,118 +155,95 @@ def tile_dot_pa_v_kernel(tc, x_crop, W_r, W_i, b_r, b_i, z, grad_out, out_0, out
                 stop=stop,
             )
 
-        def m0(h, part, jp, engs="SSSS"):
-            st = s0p.tile([P, 2, 2, D], F32, name="st0", tag="st0")
+        def m0(k, part, engs="SSSS", queue="S"):
+            h, w = hw(k)
+            st = s0p.tile([P, J, D], F32, name="st0", tag="st0")
             if part == 0:
                 plan = ((0, 0), (1, 1))
             else:
                 plan = ((1, 0), (0, 2))
-            for jj in range(2):
-                for w in range(2):
-                    k = 2 * h + w
-                    acc = mmp.tile([P, D], F32, name="acc", tag="acc")
-                    for n in range(2):
-                        dpart, wkind = plan[n]
-                        mx(acc, r[("qf", k, dpart)], P * (2 * jp + jj), E5, r[("qw", k, wkind)], E4, n == 0, n == 1)
-                    copy(
-                        engs[2 * jj + w],
-                        st[:, jj, w, :].rearrange("b (m q) -> b m q", q=J),
-                        acc[:].rearrange("b (q m) -> b m q", q=J),
-                    )
-            nc.scalar.dma_start(
-                out=o0v[:, 2 * jp : 2 * jp + 2, part, h, :], in_=st[:].rearrange("b j w c -> b j (w c)")
-            )
-
-        def m1(k, engs="SSSS"):
-            h, w = divmod(k, 2)
-            st = s1p.tile([P, J, D], F32, name="st1", tag="st1")
-            for t in range(J):
+            for j in range(J):
                 acc = mmp.tile([P, D], F32, name="acc", tag="acc")
-                for part in range(2):
-                    mx(acc, r[("qx", k, part)], P * t, E4, r[("qb", k, part)], E5, part == 0, part == 1)
-                copy(engs[t], st[:, t, :], acc[:])
-            nc.scalar.dma_start(out=o1v[:, h, w], in_=st[:])
+                for n in range(2):
+                    dpart, wkind = plan[n]
+                    mx(acc, r[("qf", k, dpart)], P * j, E5, r[("qw", k, wkind)], E4, n == 0, n == 1)
+                copy(
+                    engs[j],
+                    st[:, j, :].rearrange("b (m q) -> b m q", q=J),
+                    acc[:].rearrange("b (q m) -> b m q", q=J),
+                )
+            store(queue, o0v[:, :, part, h, w, :], st[:])
 
-        def q_f(k, part):
-            quant(("dt", k, part), ("qf", k, part), E5)
+        def store(queue, out, in_):
+            if queue == "S":
+                nc.scalar.dma_start(out=out, in_=in_)
+            else:
+                nc.sync.dma_start(out=out, in_=in_)
 
-        def q_b(k, part):
-            quant(("dni", k, part), ("qb", k, part), E5)
+        def m1(k, engs="SSSS", queue="S"):
+            h, w = hw(k)
+            for half in range(2):
+                st = s1p.tile([P, 2, D], F32, name="st1", tag="st1")
+                for tt in range(2):
+                    t = 2 * half + tt
+                    acc = mmp.tile([P, D], F32, name="acc", tag="acc")
+                    for part in range(2):
+                        mx(acc, r[("qx", k, part)], P * t, E4, r[("qb", k, part)], E5, part == 0, part == 1)
+                    copy(engs[t], st[:, tt, :], acc[:])
+                store(queue, o1v[:, h, w, 2 * half : 2 * half + 2, :], st[:])
 
-        def q_x(k, part):
-            quant(("xi", k, part), ("qx", k, part), E4)
-
-        def q_w(h):
-            for k in (2 * h, 2 * h + 1):
-                quant(("wt", k, 0), ("qw", k, 0), E4)
-                quant(("wt", k, 1), ("qw", k, 1), E4)
-                negate(k)
-            for k in (2 * h, 2 * h + 1):
-                quant(("wt", k, 2), ("qw", k, 2), E4)
-
-        def load_zg(h):
-            for part in range(2):
-                load_g(h, part)
-                load_z(h, part)
-
-        load_zg(0)
+        load_z(0, 0)
+        load_g(0)
+        load_z(0, 1)
         load_w(0, 0)
         load_w(0, 1)
-        load_x(0, 0)
-        load_x(0, 1)
-        for h in range(2):
-            a = 2 * h
-            b = a + 1
-            dz(h, 0)
-            if h == 1:
-                m1(0)
-                q_w(1)
-            turn_d(a, 0)
-            turn_d(b, 0)
-            if h == 0:
-                inter("V", "dn", a, 0)
-                inter("V", "dn", b, 0)
-            dz(h, 1)
-            if h == 1:
-                m1(1)
-            turn_d(a, 1)
-            turn_d(b, 1)
-            if h == 0:
-                q_b(a, 0)
-                q_b(b, 0)
-            q_f(a, 0)
-            q_f(b, 0)
-            if h == 0:
-                turn_w(a, 0)
-                turn_w(b, 0)
-            q_f(a, 1)
-            q_f(b, 1)
-            if h == 0:
-                turn_w(a, 1)
-                turn_w(b, 1)
-                load_w(1, 0)
-                load_w(1, 1)
-                load_zg(1)
-                q_w(0)
-            inter("S", "x", a, 1)
-            inter("S", "x", b, 1)
-            for k in (a, b):
-                m0(h, k - a, 0)
-                if h == 1:
-                    inter("V", "dn", k, 0)
-                inter("V", "dn", k, 1)
-                if h == 1:
-                    q_b(k, 0)
-                q_b(k, 1)
-                m0(h, k - a, 1)
-                inter("V", "x", k, 0)
-                q_x(k, 1)
-                q_x(k, 0)
-            if h == 0:
-                load_x(1, 0)
-                load_x(1, 1)
-                for ri in range(2):
-                    turn_w(2, ri)
-                    turn_w(3, ri)
-        m1(2, "SVSV")
-        m1(3, "SVSV")
+        load_x(0)
+        load_w(1, 0)
+        load_w(1, 1)
+        load_z(1, 0)
+        load_g(1)
+        load_z(1, 1)
+        load_x(1)
+        for k in range(NPX):
+            more = k + 2 < NPX
+            tail = "SVSV" if k == NPX - 1 else "SSSS"
+            if more:
+                load_w(k + 2, 0)
+                load_w(k + 2, 1)
+            dz(k, 0)
+            if more:
+                load_z(k + 2, 0)
+            turn(("dn", k, 0), ("dt", k, 0))
+            dz(k, 1)
+            if more:
+                load_g(k + 2)
+                load_z(k + 2, 1)
+            if k == 0:
+                turn(("w", 0, 0), ("wt", 0, 0))
+                turn(("w", 0, 1), ("wt", 0, 1))
+            turn(("dn", k, 1), ("dt", k, 1))
+            quant(("wt", k, 0), ("qw", k, 0), E4)
+            quant(("wt", k, 1), ("qw", k, 1), E4)
+            negate(k)
+            inter_x("S", k, 1)
+            inter_d("V", k, 0)
+            quant(("dt", k, 0), ("qf", k, 0), E5)
+            quant(("wt", k, 2), ("qw", k, 2), E4)
+            if k + 1 < NPX:
+                turn(("w", k + 1, 0), ("wt", k + 1, 0))
+            inter_d("V", k, 1)
+            quant(("dt", k, 1), ("qf", k, 1), E5)
+            quant(("di", k, 0), ("qb", k, 0), E5)
+            if k + 1 < NPX:
+                turn(("w", k + 1, 1), ("wt", k + 1, 1))
+            if k > 0:
+                m1(k - 1, "SSSS", "P")
+            inter_x("V", k, 0)
+            if more:
+                load_x(k + 2)
+            quant(("di", k, 1), ("qb", k, 1), E5)
+            m0(k, 0, "SSSS", "P")
+            quant(("xi", k, 1), ("qx", k, 1), E4)
+            quant(("xi", k, 0), ("qx", k, 0), E4)
+            m0(k, 1, tail, "P")
+        m1(NPX - 1, "SVSV", "P")

@@ -22,7 +22,7 @@ FLOPS = 6 * NPX * 2 * D * D * D
 
 def tile_dot_pa_v_kernel(tc, x_crop, W_r, W_i, b_r, b_i, z, grad_out, out_0, out_1):
     nc = tc.nc
-    xv = x_crop.rearrange("(p j) r h w c -> p j r h w c", j=J)
+    xv = x_crop.rearrange("(p j) r h w c -> p j r h (w c)", j=J)
     gv = grad_out.rearrange("(p j) r h w f -> p j r h w f", j=J)
     zv = z.rearrange("(p j) r h w f -> p j r h w f", j=J)
     wv = (
@@ -35,11 +35,11 @@ def tile_dot_pa_v_kernel(tc, x_crop, W_r, W_i, b_r, b_i, z, grad_out, out_0, out
     with ExitStack() as ctx:
         const = ctx.enter_context(tc.tile_pool(name="const", bufs=1))
         zp = ctx.enter_context(tc.tile_pool(name="zp", bufs=4))
-        gp = ctx.enter_context(tc.tile_pool(name="gp", bufs=2))
-        xp = ctx.enter_context(tc.tile_pool(name="xp", bufs=2))
+        gp = ctx.enter_context(tc.tile_pool(name="gp", bufs=4))
+        xp = ctx.enter_context(tc.tile_pool(name="xp", bufs=4))
         wp = ctx.enter_context(tc.tile_pool(name="wp", bufs=4))
         dnp = ctx.enter_context(tc.tile_pool(name="dnp", bufs=3))
-        ilp = ctx.enter_context(tc.tile_pool(name="ilp", bufs=3))
+        ilp = ctx.enter_context(tc.tile_pool(name="ilp", bufs=4))
         trp = ctx.enter_context(tc.tile_pool(name="trp", bufs=4))
         cwp = ctx.enter_context(tc.tile_pool(name="cwp", bufs=6))
         cdp = ctx.enter_context(tc.tile_pool(name="cdp", bufs=4))
@@ -63,17 +63,16 @@ def tile_dot_pa_v_kernel(tc, x_crop, W_r, W_i, b_r, b_i, z, grad_out, out_0, out
             nc.sync.dma_start(out=t[:], in_=zv[:, :, part, h, w, :])
             r[("z", k, part)] = t
 
-        def load_g(k):
+        def load_g(k, part):
             h, w = hw(k)
-            t = gp.tile([P, J, 2, D], BF16, name="gt", tag="gt")
-            nc.sync.dma_start(out=t[:], in_=gv[:, :, :, h, w, :])
-            r[("g", k)] = t
+            t = gp.tile([P, J, D], BF16, name="gt", tag="gt")
+            nc.sync.dma_start(out=t[:], in_=gv[:, :, part, h, w, :])
+            r[("g", k, part)] = t
 
-        def load_x(k):
-            h, w = hw(k)
-            t = xp.tile([P, J, 2, D], BF16, name="xt", tag="xt")
-            nc.sync.dma_start(out=t[:], in_=xv[:, :, :, h, w, :])
-            r[("x", k)] = t
+        def load_x(h, part):
+            t = xp.tile([P, J, 2 * D], BF16, name="xt", tag="xt")
+            nc.sync.dma_start(out=t[:], in_=xv[:, :, part, h, :])
+            r[("x", h, part)] = t
 
         def load_w(k, ri):
             h, w = hw(k)
@@ -87,7 +86,7 @@ def tile_dot_pa_v_kernel(tc, x_crop, W_r, W_i, b_r, b_i, z, grad_out, out_0, out
                 out=t[:].rearrange("p (j f) -> p j f", j=J),
                 in0=r[("z", k, part)][:],
                 scalar=0.0,
-                in1=r[("g", k)][:, :, part, :],
+                in1=r[("g", k, part)][:],
                 op0=ALU.is_gt,
                 op1=ALU.mult,
             )
@@ -142,7 +141,8 @@ def tile_dot_pa_v_kernel(tc, x_crop, W_r, W_i, b_r, b_i, z, grad_out, out_0, out
             inter(eng, r[("dn", k, part)][:].rearrange("p (j f) -> p j f", j=J), ("di", k, part))
 
         def inter_x(eng, k, part):
-            inter(eng, r[("x", k)][:, :, part, :], ("xi", k, part))
+            h, w = hw(k)
+            inter(eng, r[("x", h, part)][:, :, D * w : D * (w + 1)], ("xi", k, part))
 
         def mx(acc, lq, lo, lf, rq, rf, start, stop):
             nc.tensor.matmul_mx(
@@ -192,18 +192,18 @@ def tile_dot_pa_v_kernel(tc, x_crop, W_r, W_i, b_r, b_i, z, grad_out, out_0, out
                     copy(engs[t], st[:, tt, :], acc[:])
                 store(queue, o1v[:, h, w, 2 * half : 2 * half + 2, :], st[:])
 
-        load_z(0, 0)
-        load_g(0)
-        load_z(0, 1)
+        for part in range(2):
+            load_g(0, part)
+            load_z(0, part)
         load_w(0, 0)
         load_w(0, 1)
-        load_x(0)
+        load_x(0, 1)
+        load_x(0, 0)
         load_w(1, 0)
         load_w(1, 1)
-        load_z(1, 0)
-        load_g(1)
-        load_z(1, 1)
-        load_x(1)
+        for part in range(2):
+            load_g(1, part)
+            load_z(1, part)
         for k in range(NPX):
             more = k + 2 < NPX
             tail = "SVSV" if k == NPX - 1 else "SSSS"
@@ -212,35 +212,36 @@ def tile_dot_pa_v_kernel(tc, x_crop, W_r, W_i, b_r, b_i, z, grad_out, out_0, out
                 load_w(k + 2, 1)
             dz(k, 0)
             if more:
+                load_g(k + 2, 0)
                 load_z(k + 2, 0)
             turn(("dn", k, 0), ("dt", k, 0))
+            inter_d("V", k, 0)
             dz(k, 1)
             if more:
-                load_g(k + 2)
+                load_g(k + 2, 1)
                 load_z(k + 2, 1)
             if k == 0:
                 turn(("w", 0, 0), ("wt", 0, 0))
                 turn(("w", 0, 1), ("wt", 0, 1))
             turn(("dn", k, 1), ("dt", k, 1))
+            inter_x("S", k, 1)
+            inter_d("V", k, 1)
             quant(("wt", k, 0), ("qw", k, 0), E4)
             quant(("wt", k, 1), ("qw", k, 1), E4)
             negate(k)
-            inter_x("S", k, 1)
-            inter_d("V", k, 0)
             quant(("dt", k, 0), ("qf", k, 0), E5)
             quant(("wt", k, 2), ("qw", k, 2), E4)
+            quant(("dt", k, 1), ("qf", k, 1), E5)
             if k + 1 < NPX:
                 turn(("w", k + 1, 0), ("wt", k + 1, 0))
-            inter_d("V", k, 1)
-            quant(("dt", k, 1), ("qf", k, 1), E5)
-            quant(("di", k, 0), ("qb", k, 0), E5)
-            if k + 1 < NPX:
                 turn(("w", k + 1, 1), ("wt", k + 1, 1))
             if k > 0:
                 m1(k - 1, "SSSS", "P")
             inter_x("V", k, 0)
-            if more:
-                load_x(k + 2)
+            if k == 0:
+                load_x(1, 1)
+                load_x(1, 0)
+            quant(("di", k, 0), ("qb", k, 0), E5)
             quant(("di", k, 1), ("qb", k, 1), E5)
             m0(k, 0, "SSSS", "P")
             quant(("xi", k, 1), ("qx", k, 1), E4)

from contextlib import ExitStack

import concourse.mybir as mybir
from concourse.masks import make_identity

F32 = mybir.dt.float32
BF16 = mybir.dt.bfloat16
U32 = mybir.dt.uint32
U8 = mybir.dt.uint8
E4 = mybir.dt.float8_e4m3fn_x4
E5 = mybir.dt.float8_e5m2_x4
ALU = mybir.AluOpType

P = 128
J = 4
D = 512
NPX = 4
W4 = J * D

FLOPS = 6 * NPX * 2 * D * D * D


def tile_dot_pa_v_kernel(tc, x_crop, W_r, W_i, b_r, b_i, z, grad_out, out_0, out_1):
    nc = tc.nc
    xv = x_crop.rearrange("(p j) r h w c -> p j r h (w c)", j=J)
    gv = grad_out.rearrange("(p j) r h w f -> p j r h w f", j=J)
    zv = z.rearrange("(p j) r h w f -> p j r h w f", j=J)
    wv = (
        W_r.rearrange("h w (p q) f -> p h w q f", q=J),
        W_i.rearrange("h w (p q) f -> p h w q f", q=J),
    )
    o0v = out_0.rearrange("(p j) r h w c -> p j r h w c", j=J)
    o1v = out_1.rearrange("h w (t m) f -> m h w t f", t=J)

    with ExitStack() as ctx:
        const = ctx.enter_context(tc.tile_pool(name="const", bufs=1))
        zp = ctx.enter_context(tc.tile_pool(name="zp", bufs=4))
        gp = ctx.enter_context(tc.tile_pool(name="gp", bufs=4))
        xp = ctx.enter_context(tc.tile_pool(name="xp", bufs=4))
        wp = ctx.enter_context(tc.tile_pool(name="wp", bufs=4))
        dnp = ctx.enter_context(tc.tile_pool(name="dnp", bufs=3))
        ilp = ctx.enter_context(tc.tile_pool(name="ilp", bufs=4))
        trp = ctx.enter_context(tc.tile_pool(name="trp", bufs=4))
        cwp = ctx.enter_context(tc.tile_pool(name="cwp", bufs=6))
        cdp = ctx.enter_context(tc.tile_pool(name="cdp", bufs=4))
        s0p = ctx.enter_context(tc.tile_pool(name="s0p", bufs=3))
        s1p = ctx.enter_context(tc.tile_pool(name="s1p", bufs=4))
        tps = ctx.enter_context(tc.psum_pool(name="tps", bufs=4))
        mmp = ctx.enter_context(tc.psum_pool(name="mmp", bufs=4))
        ctx.enter_context(tc.manual_schedule())

        ident = const.tile([P, P], F32, name="ident")
        make_identity(nc, ident[:])

        r = {}

        def hw(k):
            return divmod(k, 2)

        def load_z(k, part):
            h, w = hw(k)
            t = zp.tile([P, J, D], F32, name="zt", tag="zt")
            nc.sync.dma_start(out=t[:], in_=zv[:, :, part, h, w, :])
            r[("z", k, part)] = t

        def load_g(k, part):
            h, w = hw(k)
            t = gp.tile([P, J, D], BF16, name="gt", tag="gt")
            nc.sync.dma_start(out=t[:], in_=gv[:, :, part, h, w, :])
            r[("g", k, part)] = t

        def load_x(h, part):
            t = xp.tile([P, J, 2 * D], BF16, name="xt", tag="xt")
            nc.sync.dma_start(out=t[:], in_=xv[:, :, part, h, :])
            r[("x", h, part)] = t

        def load_w(k, ri):
            h, w = hw(k)
            t = wp.tile([P, W4], BF16, name="wt", tag="wt")
            nc.sync.dma_start(out=t[:].rearrange("p (q f) -> p q f", q=J), in_=wv[ri][:, h, w])
            r[("w", k, ri)] = t

        def dz(k, part):
            t = dnp.tile([P, W4], BF16, name="dn", tag="dn", align_bytes=64)
            nc.vector.scalar_tensor_tensor(
                out=t[:].rearrange("p (j f) -> p j f", j=J),
                in0=r[("z", k, part)][:],
                scalar=0.0,
                in1=r[("g", k, part)][:],
                op0=ALU.is_gt,
                op1=ALU.mult,
            )
            r[("dn", k, part)] = t

        def copy(eng, out, in_):
            if eng == "V":
                nc.vector.tensor_copy(out=out, in_=in_)
            else:
                nc.scalar.copy(out=out, in_=in_)

        def turn(src, dst, engs="SS"):
            s = r[src]
            t = trp.tile([P, W4], BF16, name="tr", tag="tr", align_bytes=64)
            words = s[:].bitcast(F32)
            dwords = t[:].bitcast(F32)
            for half in range(2):
                bank = tps.tile([P, D], F32, name="tp", tag="tp")
                for gg in range(2):
                    g = 2 * half + gg
                    for u in range(2):
                        c = 2 * gg + u
                        nc.tensor.transpose(
                            bank[:, P * c : P * (c + 1)], words[:, 256 * g + u : 256 * (g + 1) : 2], ident[:]
                        )
                copy(
                    engs[half],
                    dwords[:, D * half : D * (half + 1)].rearrange("m (g r u) -> m g r u", g=2, u=2),
                    bank[:].rearrange("m (g u r) -> m g r u", g=2, u=2),
                )
            r[dst] = t

        def quant(src, dst, fmt):
            pool = cwp if dst[0] == "qw" else cdp
            tag = dst[0]
            codes = pool.tile([P, D], U32, name=tag + "c", tag=tag + "c", align_bytes=64)
            scales = pool.tile([P, D], U8, name=tag + "s", tag=tag + "s", align_bytes=64)
            nc.vector.quantize_mx(out=codes[:].bitcast(fmt), scales=scales[:], in_=r[src][:])
            r[dst] = (codes, scales)

        def negate(k):
            t = trp.tile([P, W4], BF16, name="tr", tag="tr", align_bytes=64)
            nc.vector.tensor_scalar_mul(t[:], r[("wt", k, 1)][:], -1.0)
            r[("wt", k, 2)] = t

        def inter(eng, src3, dst):
            t = ilp.tile([P, W4], BF16, name="il", tag="il", align_bytes=64)
            copy(eng, t[:].rearrange("p (c i j) -> p c j i", i=4, j=J), src3.rearrange("p j (c i) -> p c j i", i=4))
            r[dst] = t

        def inter_d(eng, k, part):
            inter(eng, r[("dn", k, part)][:].rearrange("p (j f) -> p j f", j=J), ("di", k, part))

        def inter_x(eng, k, part):
            h, w = hw(k)
            inter(eng, r[("x", h, part)][:, :, D * w : D * (w + 1)], ("xi", k, part))

        def mx(acc, lq, lo, lf, rq, rf, start, stop):
            nc.tensor.matmul_mx(
                out=acc[:],
                lhsT=lq[0][:, lo : lo + P].bitcast(lf),
                lhsT_scale=lq[1][:, lo : lo + P],
                rhs=rq[0][:].bitcast(rf),
                rhs_scale=rq[1][:],
                start=start,
                stop=stop,
            )

        def m0(k, part, engs="SSSS", queue="S"):
            h, w = hw(k)
            st = s0p.tile([P, J, D], F32, name="st0", tag="st0")
            if part == 0:
                plan = ((0, 0), (1, 1))
            else:
                plan = ((1, 0), (0, 2))
            for j in range(J):
                acc = mmp.tile([P, D], F32, name="acc", tag="acc")
                for n in range(2):
                    dpart, wkind = plan[n]
                    mx(acc, r[("qf", k, dpart)], P * j, E5, r[("qw", k, wkind)], E4, n == 0, n == 1)
                copy(
                    engs[j],
                    st[:, j, :].rearrange("b (m q) -> b m q", q=J),
                    acc[:].rearrange("b (q m) -> b m q", q=J),
                )
            store(queue, o0v[:, :, part, h, w, :], st[:])

        def store(queue, out, in_):
            if queue == "S":
                nc.scalar.dma_start(out=out, in_=in_)
            else:
                nc.sync.dma_start(out=out, in_=in_)

        def m1(k, engs="SSSS", queue="S"):
            h, w = hw(k)
            for half in range(2):
                st = s1p.tile([P, 2, D], F32, name="st1", tag="st1")
                for tt in range(2):
                    t = 2 * half + tt
                    acc = mmp.tile([P, D], F32, name="acc", tag="acc")
                    for part in range(2):
                        mx(acc, r[("qx", k, part)], P * t, E4, r[("qb", k, part)], E5, part == 0, part == 1)
                    copy(engs[t], st[:, tt, :], acc[:])
                store(queue, o1v[:, h, w, 2 * half : 2 * half + 2, :], st[:])

        for part in range(2):
            load_g(0, part)
            load_z(0, part)
        load_w(0, 0)
        load_w(0, 1)
        load_x(0, 1)
        load_x(0, 0)
        load_w(1, 0)
        load_w(1, 1)
        for part in range(2):
            load_g(1, part)
            load_z(1, part)
        for k in range(NPX):
            more = k + 2 < NPX
            tail = "SVSV" if k == NPX - 1 else "SSSS"
            if more:
                load_w(k + 2, 0)
                load_w(k + 2, 1)
            dz(k, 0)
            if more:
                load_g(k + 2, 0)
                load_z(k + 2, 0)
            turn(("dn", k, 0), ("dt", k, 0))
            inter_d("V", k, 0)
            dz(k, 1)
            if more:
                load_g(k + 2, 1)
                load_z(k + 2, 1)
            if k == 0:
                turn(("w", 0, 0), ("wt", 0, 0))
                turn(("w", 0, 1), ("wt", 0, 1))
            turn(("dn", k, 1), ("dt", k, 1))
            inter_x("S", k, 1)
            inter_d("V", k, 1)
            quant(("wt", k, 0), ("qw", k, 0), E4)
            quant(("wt", k, 1), ("qw", k, 1), E4)
            negate(k)
            quant(("dt", k, 0), ("qf", k, 0), E5)
            quant(("wt", k, 2), ("qw", k, 2), E4)
            quant(("dt", k, 1), ("qf", k, 1), E5)
            if k + 1 < NPX:
                turn(("w", k + 1, 0), ("wt", k + 1, 0))
                turn(("w", k + 1, 1), ("wt", k + 1, 1))
            if k > 0:
                m1(k - 1, "SSSS", "P")
            inter_x("V", k, 0)
            if k == 0:
                load_x(1, 1)
                load_x(1, 0)
            quant(("di", k, 0), ("qb", k, 0), E5)
            quant(("di", k, 1), ("qb", k, 1), E5)
            m0(k, 0, "SSSS", "P")
            quant(("xi", k, 1), ("qx", k, 1), E4)
            quant(("xi", k, 0), ("qx", k, 0), E4)
            m0(k, 1, tail, "P")
        m1(NPX - 1, "SVSV", "P")
